import numpy as np
import ml_dtypes


def mxq(x, axis, fmt="e4m3"):
    dtype, down = {"e4m3": (ml_dtypes.float8_e4m3fn, 7), "e5m2": (ml_dtypes.float8_e5m2, 14)}[fmt]
    v = np.moveaxis(np.asarray(x, np.float32).astype(ml_dtypes.bfloat16).astype(np.float64), axis, -1)
    blocks = v.reshape(v.shape[:-1] + (-1, 32))
    amax = np.abs(blocks).max(-1, keepdims=True)
    byte = np.maximum(np.where(amax > 0, np.frexp(amax)[1] - 1 + 127, 0) - down, 1)
    scale = np.exp2(byte - 127.0)
    codes = (blocks / scale).astype(np.float32).astype(dtype).astype(np.float64)
    return np.moveaxis((codes * scale).reshape(v.shape), -1, axis)


WIDE = False


def mx_kscale(k):
    if not WIDE:
        return np.ones(k)
    levels = np.array([10, -10, 5, -5, 0])
    if k % 512:
        return np.exp2(np.random.permutation(np.resize(levels, k // 32))).repeat(32)
    a = np.empty((k // 512, 16))
    for p in range(k // 512):
        a[p, :8] = np.random.permutation(np.resize(levels, 8))
        for g in range(8):
            far = levels[np.abs(levels - a[p, g]) >= 10]
            a[p, g + 8] = far[np.random.randint(len(far))]
    return np.exp2(a.ravel()).repeat(32)


BF16 = ml_dtypes.bfloat16


def bf(x):
    return np.asarray(x, np.float32).astype(BF16)


def f64(x):
    return np.asarray(x).astype(np.float64)


B, L, E, H, HD, F, G = 4, 128, 1024, 8, 128, 2048, 2048


def sigmoid(v):
    return 1.0 / (1.0 + np.exp(-v))


def setup_inputs():
    s, t = mx_kscale(E), mx_kscale(F)
    return {"h_ffn": bf(np.random.standard_normal((B, L, E)) * s),
            "w1": bf(np.random.standard_normal((E, F)) / np.sqrt(E) / s[:, None] * t),
            "b1": bf(0.2 * np.random.standard_normal(F) * t),
            "wg": bf(np.random.standard_normal((F, G)) / np.sqrt(F) / t[:, None]),
            "bg": bf(0.2 * np.random.standard_normal(G)),
            "wl": bf(np.random.standard_normal((F, G)) / np.sqrt(F) / t[:, None]),
            "bl": bf(0.2 * np.random.standard_normal(G)),
            "beta": bf(1.5 + 0.1 * np.random.standard_normal(1))}


def reference(h_ffn, w1, b1, wg, bg, wl, bl, beta):
    u = (mxq(f64(h_ffn), 2, "e4m3") @ mxq(f64(w1), 0, "e4m3")) + f64(b1)
    uq = mxq(u, 2, "e4m3")
    gate = (uq @ mxq(f64(wg), 0, "e4m3")) + f64(bg)
    lin = (uq @ mxq(f64(wl), 0, "e4m3")) + f64(bl)
    return gate * sigmoid(f64(beta) * gate) * lin

@@ -1,0 +1,322 @@
+from contextlib import ExitStack
+
+import concourse.mybir as mybir
+from concourse.masks import make_identity
+
+BF16 = mybir.dt.bfloat16
+F32 = mybir.dt.float32
+U32 = mybir.dt.uint32
+U8 = mybir.dt.uint8
+FP8X4 = mybir.dt.float8_e4m3fn_x4
+ACT = mybir.ActivationFunctionType
+ALU = mybir.AluOpType
+
+P = 128
+PACK = 4
+K_PASS = P * PACK
+
+BATCH = 4
+TOKENS = BATCH * P
+E = 1024
+F = 2048
+G = 2048
+E_PASSES = E // K_PASS
+F_PASSES = F // K_PASS
+
+QUANT = 4096
+WORDS = QUANT // PACK
+STRIPS_PER_LOAD = 4
+RAW = STRIPS_PER_LOAD * QUANT
+RAW_BUFS = 3
+BANKS = 8
+TILES_PER_STRIP = WORDS // F_PASSES // P
+
+QUANTISE_LAG = 1
+MULTIPLY_LAG = 2
+SIGMOID_LAG = 3
+FINISH_LAG = 3
+TURN_LAG = 4
+STORE_LAG = 4
+
+FLOPS = 2 * TOKENS * E * F + 2 * 2 * TOKENS * F * G
+
+
+def tile_llamaselfattentionblock_pb_kernel(tc, h_ffn, w1, b1, wg, bg, wl, bl, beta, out):
+    nc = tc.nc
+    with ExitStack() as ctx:
+        const = ctx.enter_context(tc.tile_pool(name="const", bufs=1))
+        raw_pool = ctx.enter_context(tc.tile_pool(name="raw", bufs=RAW_BUFS))
+        grouped_pool = ctx.enter_context(tc.tile_pool(name="grouped", bufs=3))
+        strip_pool = ctx.enter_context(tc.tile_pool(name="strip", bufs=4))
+        u_pool = ctx.enter_context(tc.tile_pool(name="u", bufs=2))
+        swish_pool = ctx.enter_context(tc.tile_pool(name="swish", bufs=10))
+        work = ctx.enter_context(tc.tile_pool(name="work", bufs=4))
+        out_pool = ctx.enter_context(tc.tile_pool(name="out", bufs=2))
+        psum = ctx.enter_context(tc.psum_pool(name="psum", bufs=BANKS))
+        ctx.enter_context(tc.manual_schedule())
+        loads = [("u", w1, 0)]
+        for half in range(2):
+            loads.append(("gate", wg, half))
+            loads.append(("lin", wl, half))
+        n_strips = len(loads) * STRIPS_PER_LOAD
+
+        def kind(i):
+            return loads[i // STRIPS_PER_LOAD][0] if 0 <= i < n_strips else "none"
+
+        raw_of = {}
+        grouped_of = {}
+        words_of = {}
+        scales_of = {}
+        acc_of = {}
+        sig_of = {}
+        swish_of = {}
+        prod_of = {}
+        turned_of = {}
+
+        def load(s):
+            w, half = loads[s][1], loads[s][2]
+            rows = w.shape[0] // P
+            width = RAW // rows
+            raw = raw_pool.tile([P, rows, width], BF16, tag="raw")
+            cuts = max(1, STRIPS_PER_LOAD >> s)
+            piece = width // cuts
+            for cut in range(cuts):
+                first = half * width + cut * piece
+                for g in range(rows // PACK):
+                    nc.sync.dma_start(
+                        out=raw[:, g * PACK : (g + 1) * PACK, cut * piece : (cut + 1) * piece],
+                        in_=w[g * K_PASS : (g + 1) * K_PASS, first : first + piece].rearrange("(p t) n -> p t n", t=PACK),
+                    )
+            raw_of[s] = raw
+
+        def regroup(i):
+            s, q = divmod(i, STRIPS_PER_LOAD)
+            raw = raw_of[s]
+            passes = raw.shape[1] // PACK
+            n = WORDS // passes
+            vector_passes = 0 if kind(i - FINISH_LAG) == "u" else passes // 2
+            grouped = grouped_pool.tile([P, passes, n, PACK], BF16, align_bytes=64, tag="grouped")
+            cols = slice(q * n, (q + 1) * n)
+            if kind(i) == "u":
+                for g in range(passes):
+                    copy = nc.vector.tensor_copy if g < vector_passes else nc.scalar.copy
+                    copy(
+                        out=grouped[:, g, :, :].rearrange("p (a m) t -> p a m t", a=PACK),
+                        in_=raw[:, g * PACK : (g + 1) * PACK, cols].rearrange("p t (m a) -> p a m t", a=PACK),
+                    )
+                vector_passes = passes
+            elif vector_passes > 0:
+                nc.vector.tensor_copy(
+                    out=grouped[:, 0:vector_passes, :, :].rearrange("p g (c i) t -> p g c t i", i=4),
+                    in_=raw[:, 0 : vector_passes * PACK, cols].rearrange("p (g t) (c i) -> p g c t i", t=PACK, i=4),
+                )
+            for g in range(vector_passes, passes):
+                nc.scalar.copy(
+                    out=grouped[:, g, :, :].rearrange("p (c i) t -> p c t i", i=4),
+                    in_=raw[:, g * PACK : (g + 1) * PACK, cols].rearrange("p t (c i) -> p c t i", i=4),
+                )
+            grouped_of[i] = grouped
+            if q == STRIPS_PER_LOAD - 1 and s + RAW_BUFS < len(loads):
+                load(s + RAW_BUFS)
+
+        def quantise(i):
+            grouped = grouped_of[i]
+            passes, n = grouped.shape[1], grouped.shape[2]
+            words = strip_pool.tile([P, passes, n], U32, align_bytes=64, tag="words")
+            scales = strip_pool.tile([P, passes, n], U8, align_bytes=64, tag="scales")
+            nc.vector.quantize_mx(
+                out=words[:].rearrange("p g n -> p (g n)").bitcast(FP8X4),
+                scales=scales[:].rearrange("p g n -> p (g n)"),
+                in_=grouped[:].rearrange("p g n t -> p (g n t)"),
+            )
+            words_of[i] = words
+            scales_of[i] = scales
+
+        def column_tile(i, j):
+            s, q = divmod(i, STRIPS_PER_LOAD)
+            return (loads[s][2] * STRIPS_PER_LOAD + q) * TILES_PER_STRIP + j
+
+        def multiply(i):
+            words, scales = words_of[i], scales_of[i]
+            banks = []
+            if kind(i) == "u":
+                for b in range(BATCH):
+                    tokens = slice(b * P, (b + 1) * P)
+                    u_acc = psum.tile([P, PACK, P], F32, tag="bank")
+                    for t in range(PACK):
+                        features = slice(t * P, (t + 1) * P)
+                        for c in range(E_PASSES):
+                            nc.tensor.matmul_mx(
+                                out=u_acc[:, t, :],
+                                lhsT=words[:, c, features].bitcast(FP8X4),
+                                lhsT_scale=scales[:, c, features],
+                                rhs=h_words[:, c, tokens].bitcast(FP8X4),
+                                rhs_scale=h_scales[:, c, tokens],
+                                start=(c == 0),
+                                stop=(c == E_PASSES - 1),
+                            )
+                    banks.append(u_acc)
+            else:
+                for j in range(TILES_PER_STRIP):
+                    cols = slice(j * P, (j + 1) * P)
+                    acc = psum.tile([P, TOKENS], F32, tag="bank")
+                    for g in range(F_PASSES):
+                        nc.tensor.matmul_mx(
+                            out=acc[:],
+                            lhsT=words[:, g, cols].bitcast(FP8X4),
+                            lhsT_scale=scales[:, g, cols],
+                            rhs=u_words[:, g, :].bitcast(FP8X4),
+                            rhs_scale=u_scales[:, g, :],
+                            start=(g == 0),
+                            stop=(g == F_PASSES - 1),
+                        )
+                    banks.append(acc)
+            acc_of[i] = banks
+
+        def sigmoid(i):
+            sigs = []
+            for j in range(TILES_PER_STRIP):
+                m = column_tile(i, j)
+                sig = work.tile([P, TOKENS], F32, tag="sig")
+                nc.scalar.activation(
+                    out=sig[:],
+                    in_=acc_of[i][j][:],
+                    func=ACT.Sigmoid,
+                    bias=beta_bg_cols[:, m : m + 1],
+                    scale=beta_col[:, 0:1],
+                )
+                sigs.append(sig)
+            sig_of[i] = sigs
+
+        def finish(i):
+            if kind(i) == "u":
+                u_grouped = u_pool.tile([P, TOKENS, PACK], BF16, align_bytes=64)
+                for b in range(BATCH):
+                    nc.vector.tensor_tensor(
+                        out=u_grouped[:, b * P : (b + 1) * P, :],
+                        in0=acc_of[i][b][:].rearrange("p t r -> p r t"),
+                        in1=b1_cols[:, i * PACK : (i + 1) * PACK].unsqueeze(1).to_broadcast([P, P, PACK]),
+                        op=ALU.add,
+                    )
+                nc.vector.quantize_mx(
+                    out=u_words[:, i, :].bitcast(FP8X4),
+                    scales=u_scales[:, i, :],
+                    in_=u_grouped[:].rearrange("p r t -> p (r t)"),
+                )
+            elif kind(i) == "gate":
+                swishes = []
+                for j in range(TILES_PER_STRIP):
+                    m = column_tile(i, j)
+                    swish = swish_pool.tile([P, TOKENS], F32)
+                    nc.vector.scalar_tensor_tensor(
+                        out=swish[:], in0=acc_of[i][j][:], scalar=bg_cols[:, m : m + 1], in1=sig_of[i][j][:],
+                        op0=ALU.add, op1=ALU.mult,
+                    )
+                    swishes.append(swish)
+                swish_of[i] = swishes
+            else:
+                prods = []
+                for j in range(TILES_PER_STRIP):
+                    m = column_tile(i, j)
+                    prod = work.tile([P, TOKENS], F32, tag="prod")
+                    nc.vector.scalar_tensor_tensor(
+                        out=prod[:], in0=acc_of[i][j][:], scalar=bl_cols[:, m : m + 1],
+                        in1=swish_of[i - STRIPS_PER_LOAD][j][:], op0=ALU.add, op1=ALU.mult,
+                    )
+                    prods.append(prod)
+                prod_of[i] = prods
+
+        def turn(i):
+            banks = []
+            for j in range(TILES_PER_STRIP):
+                turned = psum.tile([P, BATCH, P], F32, tag="bank")
+                for b in range(BATCH):
+                    nc.tensor.transpose(
+                        out=turned[:, b, :], in_=prod_of[i][j][:, b * P : (b + 1) * P], identity=ident_f32[:]
+                    )
+                banks.append(turned)
+            turned_of[i] = banks
+
+        def store(i):
+            out_sb = out_pool.tile([P, BATCH, TILES_PER_STRIP * P], F32)
+            for j in range(TILES_PER_STRIP):
+                nc.scalar.copy(out=out_sb[:, :, j * P : (j + 1) * P], in_=turned_of[i][j][:])
+            first = column_tile(i, 0) * P
+            nc.sync.dma_start(out=out_view[:, :, first : first + TILES_PER_STRIP * P], in_=out_sb[:])
+
+        tiles_g = G // P
+        bias_rows = const.tile([P, P], BF16)
+        nc.vector.memset(bias_rows[:], 0.0)
+        nc.sync.dma_start(out=bias_rows[0:tiles_g, :], in_=bg.rearrange("(m p) -> m p", p=P))
+        nc.sync.dma_start(out=bias_rows[tiles_g : 2 * tiles_g, :], in_=bl.rearrange("(m p) -> m p", p=P))
+        b1_bf16 = const.tile([P, F_PASSES, PACK], BF16)
+        nc.scalar.dma_start(out=b1_bf16[:], in_=b1.rearrange("(i p t) -> p i t", p=P, t=PACK))
+        beta_bf16 = const.tile([P, 1], BF16)
+        nc.sync.dma_start(out=beta_bf16[:], in_=beta.partition_broadcast(P))
+
+        h_raw = const.tile([P, BATCH, E], BF16)
+        for b in range(BATCH):
+            nc.sync.dma_start(out=h_raw[:, b, :], in_=h_ffn[b, :, :])
+        for s in range(RAW_BUFS):
+            load(s)
+        out_view = out.rearrange("b l n -> l b n")
+
+        warm = const.tile([P, 1], F32)
+        nc.vector.memset(warm[:], 0.0)
+        nc.scalar.activation(out=warm[:], in_=warm[:], func=ACT.Sigmoid)
+
+        ident_bf16 = const.tile([P, P], BF16)
+        make_identity(nc, ident_bf16[:])
+        ident_f32 = const.tile([P, P], F32)
+        make_identity(nc, ident_f32[:])
+
+        h_grouped = grouped_pool.tile([P, E_PASSES, TOKENS, PACK], BF16, align_bytes=64, tag="grouped")
+        for c in range(E_PASSES):
+            for b in range(BATCH):
+                h_t = psum.tile([P, PACK, P], BF16, tag="bank")
+                for t in range(PACK):
+                    k0 = c * K_PASS
+                    nc.tensor.transpose(
+                        out=h_t[:, t, :], in_=h_raw[:, b, k0 + t : k0 + K_PASS : PACK], identity=ident_bf16[:]
+                    )
+                copy = nc.vector.tensor_copy if b % 2 == 0 else nc.scalar.copy
+                copy(out=h_grouped[:, c, b * P : (b + 1) * P, :], in_=h_t[:].rearrange("p t r -> p r t"))
+        h_words = const.tile([P, E_PASSES, TOKENS], U32, align_bytes=64)
+        h_scales = const.tile([P, E_PASSES, TOKENS], U8, align_bytes=64)
+        nc.vector.quantize_mx(
+            out=h_words[:].rearrange("p c r -> p (c r)").bitcast(FP8X4),
+            scales=h_scales[:].rearrange("p c r -> p (c r)"),
+            in_=h_grouped[:].rearrange("p c r t -> p (c r t)"),
+        )
+
+        bias_t = psum.tile([P, P], BF16, tag="bank")
+        nc.tensor.transpose(out=bias_t[:], in_=bias_rows[:], identity=ident_bf16[:])
+        bias_cols = const.tile([P, 2 * tiles_g], F32)
+        nc.vector.tensor_copy(out=bias_cols[:], in_=bias_t[:, 0 : 2 * tiles_g])
+        b1_cols = const.tile([P, F_PASSES * PACK], F32)
+        nc.vector.tensor_copy(out=b1_cols[:], in_=b1_bf16[:].rearrange("p i t -> p (i t)"))
+        bg_cols = bias_cols[:, 0:tiles_g]
+        bl_cols = bias_cols[:, tiles_g : 2 * tiles_g]
+        beta_col = const.tile([P, 1], F32)
+        nc.vector.tensor_copy(out=beta_col[:], in_=beta_bf16[:])
+        beta_bg_cols = const.tile([P, tiles_g], F32)
+        nc.vector.tensor_scalar_mul(out=beta_bg_cols[:], in0=bg_cols, scalar1=beta_col[:, 0:1])
+
+        u_words = const.tile([P, F_PASSES, TOKENS], U32, align_bytes=64)
+        u_scales = const.tile([P, F_PASSES, TOKENS], U8, align_bytes=64)
+
+        for step in range(n_strips + STORE_LAG):
+            if kind(step - TURN_LAG) == "lin":
+                turn(step - TURN_LAG)
+            if kind(step - SIGMOID_LAG) == "gate":
+                sigmoid(step - SIGMOID_LAG)
+            if kind(step) != "none":
+                regroup(step)
+            if kind(step - STORE_LAG) == "lin":
+                store(step - STORE_LAG)
+            if kind(step - FINISH_LAG) != "none":
+                finish(step - FINISH_LAG)
+            if kind(step - QUANTISE_LAG) != "none":
+                quantise(step - QUANTISE_LAG)
+            if kind(step - MULTIPLY_LAG) != "none":
+                multiply(step - MULTIPLY_LAG)

@@ -26,14 +26,14 @@ F_PASSES = F // K_PASS
 QUANT = 4096
 WORDS = QUANT // PACK
 STRIPS_PER_LOAD = 4
-RAW = STRIPS_PER_LOAD * QUANT
-RAW_BUFS = 3
+PIECE = 4096
+PIECE_BUFS = 13
 BANKS = 8
 TILES_PER_STRIP = WORDS // F_PASSES // P
 
 QUANTISE_LAG = 1
 MULTIPLY_LAG = 2
-SIGMOID_LAG = 3
+SILU_LAG = 3
 FINISH_LAG = 3
 TURN_LAG = 4
 STORE_LAG = 4
@@ -45,11 +45,11 @@ def tile_llamaselfattentionblock_pb_kernel(tc, h_ffn, w1, b1, wg, bg, wl, bl, be
     nc = tc.nc
     with ExitStack() as ctx:
         const = ctx.enter_context(tc.tile_pool(name="const", bufs=1))
-        raw_pool = ctx.enter_context(tc.tile_pool(name="raw", bufs=RAW_BUFS))
+        raw_pool = ctx.enter_context(tc.tile_pool(name="raw", bufs=PIECE_BUFS))
         grouped_pool = ctx.enter_context(tc.tile_pool(name="grouped", bufs=3))
         strip_pool = ctx.enter_context(tc.tile_pool(name="strip", bufs=4))
         u_pool = ctx.enter_context(tc.tile_pool(name="u", bufs=2))
-        swish_pool = ctx.enter_context(tc.tile_pool(name="swish", bufs=10))
+        silu_pool = ctx.enter_context(tc.tile_pool(name="silu", bufs=12))
         work = ctx.enter_context(tc.tile_pool(name="work", bufs=4))
         out_pool = ctx.enter_context(tc.tile_pool(name="out", bufs=2))
         psum = ctx.enter_context(tc.psum_pool(name="psum", bufs=BANKS))
@@ -68,56 +68,73 @@ def tile_llamaselfattentionblock_pb_kernel(tc, h_ffn, w1, b1, wg, bg, wl, bl, be
         words_of = {}
         scales_of = {}
         acc_of = {}
-        sig_of = {}
-        swish_of = {}
+        silu_of = {}
         prod_of = {}
         turned_of = {}
 
-        def load(s):
-            w, half = loads[s][1], loads[s][2]
-            rows = w.shape[0] // P
-            width = RAW // rows
-            raw = raw_pool.tile([P, rows, width], BF16, tag="raw")
-            cuts = max(1, STRIPS_PER_LOAD >> s)
-            piece = width // cuts
-            for cut in range(cuts):
-                first = half * width + cut * piece
-                for g in range(rows // PACK):
-                    nc.sync.dma_start(
-                        out=raw[:, g * PACK : (g + 1) * PACK, cut * piece : (cut + 1) * piece],
-                        in_=w[g * K_PASS : (g + 1) * K_PASS, first : first + piece].rearrange("(p t) n -> p t n", t=PACK),
-                    )
-            raw_of[s] = raw
+        pieces = []
+        for s, (what, w, half) in enumerate(loads):
+            passes = w.shape[0] // K_PASS
+            width = STRIPS_PER_LOAD * WORDS // passes
+            group = 2 if s < 2 else 1
+            columns = PIECE // PACK // group
+            for c in range(half * width, (half + 1) * width, columns):
+                for g in range(0, passes, group):
+                    pieces.append((s, g, group, c, columns))
+
+        def strip_columns(i):
+            s, q = divmod(i, STRIPS_PER_LOAD)
+            n = WORDS // (loads[s][1].shape[0] // K_PASS)
+            return (loads[s][2] * STRIPS_PER_LOAD + q) * n, n
+
+        def last_strip(piece):
+            s, g, group, c, columns = piece
+            first, n = strip_columns(s * STRIPS_PER_LOAD)
+            return s * STRIPS_PER_LOAD + (c + columns - first) // n - 1
+
+        def load(piece):
+            s, g, group, c, columns = piece
+            w = loads[s][1]
+            raw = raw_pool.tile([P, group * PACK, columns], BF16, tag="raw")
+            for k in range(group):
+                nc.sync.dma_start(
+                    out=raw[:, k * PACK : (k + 1) * PACK, :],
+                    in_=w[(g + k) * K_PASS : (g + k + 1) * K_PASS, c : c + columns].rearrange("(p t) n -> p t n", t=PACK),
+                )
+                for i in range(s * STRIPS_PER_LOAD, (s + 1) * STRIPS_PER_LOAD):
+                    first, n = strip_columns(i)
+                    if c <= first < c + columns:
+                        raw_of[i, g + k] = (raw, k * PACK, first - c)
+
+        loaded = []
+
+        def load_ahead(done):
+            while len(loaded) < len(pieces) and sum(last_strip(p) >= done for p in loaded) < PIECE_BUFS:
+                load(pieces[len(loaded)])
+                loaded.append(pieces[len(loaded)])
 
         def regroup(i):
-            s, q = divmod(i, STRIPS_PER_LOAD)
-            raw = raw_of[s]
-            passes = raw.shape[1] // PACK
-            n = WORDS // passes
-            vector_passes = 0 if kind(i - FINISH_LAG) == "u" else passes // 2
+            first, n = strip_columns(i)
+            passes = WORDS // n
+            quarters = {"none": 2, "u": 0, "gate": 3, "lin": 2}[kind(i - FINISH_LAG)]
+            vector_passes = quarters * passes // 4
             grouped = grouped_pool.tile([P, passes, n, PACK], BF16, align_bytes=64, tag="grouped")
-            cols = slice(q * n, (q + 1) * n)
-            if kind(i) == "u":
-                for g in range(passes):
-                    copy = nc.vector.tensor_copy if g < vector_passes else nc.scalar.copy
+            for g in range(passes):
+                raw, row, col = raw_of[i, g]
+                rows = raw[:, row : row + PACK, col : col + n]
+                copy = nc.vector.tensor_copy if g < vector_passes else nc.scalar.copy
+                if kind(i) == "u":
                     copy(
                         out=grouped[:, g, :, :].rearrange("p (a m) t -> p a m t", a=PACK),
-                        in_=raw[:, g * PACK : (g + 1) * PACK, cols].rearrange("p t (m a) -> p a m t", a=PACK),
+                        in_=rows.rearrange("p t (m a) -> p a m t", a=PACK),
                     )
-                vector_passes = passes
-            elif vector_passes > 0:
-                nc.vector.tensor_copy(
-                    out=grouped[:, 0:vector_passes, :, :].rearrange("p g (c i) t -> p g c t i", i=4),
-                    in_=raw[:, 0 : vector_passes * PACK, cols].rearrange("p (g t) (c i) -> p g c t i", t=PACK, i=4),
-                )
-            for g in range(vector_passes, passes):
-                nc.scalar.copy(
-                    out=grouped[:, g, :, :].rearrange("p (c i) t -> p c t i", i=4),
-                    in_=raw[:, g * PACK : (g + 1) * PACK, cols].rearrange("p t (c i) -> p c t i", i=4),
-                )
+                else:
+                    copy(
+                        out=grouped[:, g, :, :].rearrange("p (c i) t -> p c t i", i=4),
+                        in_=rows.rearrange("p t (c i) -> p c t i", i=4),
+                    )
             grouped_of[i] = grouped
-            if q == STRIPS_PER_LOAD - 1 and s + RAW_BUFS < len(loads):
-                load(s + RAW_BUFS)
+            load_ahead(i + 1)
 
         def quantise(i):
             grouped = grouped_of[i]
@@ -173,20 +190,20 @@ def tile_llamaselfattentionblock_pb_kernel(tc, h_ffn, w1, b1, wg, bg, wl, bl, be
                     banks.append(acc)
             acc_of[i] = banks
 
-        def sigmoid(i):
-            sigs = []
+        def silu(i):
+            silus = []
             for j in range(TILES_PER_STRIP):
                 m = column_tile(i, j)
-                sig = work.tile([P, TOKENS], F32, tag="sig")
+                y = silu_pool.tile([P, TOKENS], F32)
                 nc.scalar.activation(
-                    out=sig[:],
+                    out=y[:],
                     in_=acc_of[i][j][:],
-                    func=ACT.Sigmoid,
+                    func=ACT.Silu,
                     bias=beta_bg_cols[:, m : m + 1],
                     scale=beta_col[:, 0:1],
                 )
-                sigs.append(sig)
-            sig_of[i] = sigs
+                silus.append(y)
+            silu_of[i] = silus
 
         def finish(i):
             if kind(i) == "u":
@@ -203,25 +220,14 @@ def tile_llamaselfattentionblock_pb_kernel(tc, h_ffn, w1, b1, wg, bg, wl, bl, be
                     scales=u_scales[:, i, :],
                     in_=u_grouped[:].rearrange("p r t -> p (r t)"),
                 )
-            elif kind(i) == "gate":
-                swishes = []
-                for j in range(TILES_PER_STRIP):
-                    m = column_tile(i, j)
-                    swish = swish_pool.tile([P, TOKENS], F32)
-                    nc.vector.scalar_tensor_tensor(
-                        out=swish[:], in0=acc_of[i][j][:], scalar=bg_cols[:, m : m + 1], in1=sig_of[i][j][:],
-                        op0=ALU.add, op1=ALU.mult,
-                    )
-                    swishes.append(swish)
-                swish_of[i] = swishes
-            else:
+            elif kind(i) == "lin":
                 prods = []
                 for j in range(TILES_PER_STRIP):
                     m = column_tile(i, j)
                     prod = work.tile([P, TOKENS], F32, tag="prod")
                     nc.vector.scalar_tensor_tensor(
                         out=prod[:], in0=acc_of[i][j][:], scalar=bl_cols[:, m : m + 1],
-                        in1=swish_of[i - STRIPS_PER_LOAD][j][:], op0=ALU.add, op1=ALU.mult,
+                        in1=silu_of[i - STRIPS_PER_LOAD][j][:], op0=ALU.add, op1=ALU.mult,
                     )
                     prods.append(prod)
                 prod_of[i] = prods
@@ -240,7 +246,9 @@ def tile_llamaselfattentionblock_pb_kernel(tc, h_ffn, w1, b1, wg, bg, wl, bl, be
         def store(i):
             out_sb = out_pool.tile([P, BATCH, TILES_PER_STRIP * P], F32)
             for j in range(TILES_PER_STRIP):
-                nc.scalar.copy(out=out_sb[:, :, j * P : (j + 1) * P], in_=turned_of[i][j][:])
+                nc.scalar.activation(
+                    out=out_sb[:, :, j * P : (j + 1) * P], in_=turned_of[i][j][:], func=ACT.Copy, scale=inv_beta_col[:, 0:1]
+                )
             first = column_tile(i, 0) * P
             nc.sync.dma_start(out=out_view[:, :, first : first + TILES_PER_STRIP * P], in_=out_sb[:])
 
@@ -257,13 +265,12 @@ def tile_llamaselfattentionblock_pb_kernel(tc, h_ffn, w1, b1, wg, bg, wl, bl, be
         h_raw = const.tile([P, BATCH, E], BF16)
         for b in range(BATCH):
             nc.sync.dma_start(out=h_raw[:, b, :], in_=h_ffn[b, :, :])
-        for s in range(RAW_BUFS):
-            load(s)
+        load_ahead(0)
         out_view = out.rearrange("b l n -> l b n")
 
         warm = const.tile([P, 1], F32)
         nc.vector.memset(warm[:], 0.0)
-        nc.scalar.activation(out=warm[:], in_=warm[:], func=ACT.Sigmoid)
+        nc.scalar.activation(out=warm[:], in_=warm[:], func=ACT.Silu)
 
         ident_bf16 = const.tile([P, P], BF16)
         make_identity(nc, ident_bf16[:])
@@ -297,8 +304,23 @@ def tile_llamaselfattentionblock_pb_kernel(tc, h_ffn, w1, b1, wg, bg, wl, bl, be
         nc.vector.tensor_copy(out=b1_cols[:], in_=b1_bf16[:].rearrange("p i t -> p (i t)"))
         bg_cols = bias_cols[:, 0:tiles_g]
         bl_cols = bias_cols[:, tiles_g : 2 * tiles_g]
+        beta_f32 = const.tile([P, 1], F32)
+        nc.vector.tensor_copy(out=beta_f32[:], in_=beta_bf16[:])
+        beta_sign = const.tile([P, 1], F32)
+        nc.vector.tensor_scalar(out=beta_sign[:], in0=beta_f32[:], scalar1=0.0, scalar2=2.0, op0=ALU.is_ge, op1=ALU.mult)
+        beta_abs = const.tile([P, 1], F32)
+        nc.vector.scalar_tensor_tensor(
+            out=beta_abs[:], in0=beta_f32[:], scalar=-1.0, in1=beta_f32[:], op0=ALU.mult, op1=ALU.max
+        )
+        nc.vector.tensor_scalar(
+            out=beta_abs[:], in0=beta_abs[:], scalar1=2.0**-30, scalar2=2.0**64, op0=ALU.max, op1=ALU.min
+        )
         beta_col = const.tile([P, 1], F32)
-        nc.vector.tensor_copy(out=beta_col[:], in_=beta_bf16[:])
+        nc.vector.scalar_tensor_tensor(
+            out=beta_col[:], in0=beta_sign[:], scalar=-1.0, in1=beta_abs[:], op0=ALU.add, op1=ALU.mult
+        )
+        inv_beta_col = const.tile([P, 1], F32)
+        nc.vector.reciprocal(out=inv_beta_col[:], in_=beta_col[:])
         beta_bg_cols = const.tile([P, tiles_g], F32)
         nc.vector.tensor_scalar_mul(out=beta_bg_cols[:], in0=bg_cols, scalar1=beta_col[:, 0:1])
 
@@ -308,8 +330,8 @@ def tile_llamaselfattentionblock_pb_kernel(tc, h_ffn, w1, b1, wg, bg, wl, bl, be
         for step in range(n_strips + STORE_LAG):
             if kind(step - TURN_LAG) == "lin":
                 turn(step - TURN_LAG)
-            if kind(step - SIGMOID_LAG) == "gate":
-                sigmoid(step - SIGMOID_LAG)
+            if kind(step - SILU_LAG) == "gate":
+                silu(step - SILU_LAG)
             if kind(step) != "none":
                 regroup(step)
             if kind(step - STORE_LAG) == "lin":

@@ -13,6 +13,7 @@ ALU = mybir.AluOpType
 
 P = 128
 PACK = 4
+PAIR = 2
 K_PASS = P * PACK
 
 BATCH = 4
@@ -23,20 +24,17 @@ G = 2048
 E_PASSES = E // K_PASS
 F_PASSES = F // K_PASS
 
-QUANT = 4096
-WORDS = QUANT // PACK
-STRIPS_PER_LOAD = 4
+HALF = G // 2
 PIECE = 4096
 PIECE_BUFS = 13
 BANKS = 8
-TILES_PER_STRIP = WORDS // F_PASSES // P
 
 QUANTISE_LAG = 1
 MULTIPLY_LAG = 2
-SILU_LAG = 3
 FINISH_LAG = 3
 TURN_LAG = 4
-STORE_LAG = 4
+
+VECTOR_QUARTERS = {"none": 2.0, "u": 0.5, "gate": 2.5, "lin": 2.0}
 
 FLOPS = 2 * TOKENS * E * F + 2 * 2 * TOKENS * F * G
 
@@ -54,14 +52,19 @@ def tile_llamaselfattentionblock_pb_kernel(tc, h_ffn, w1, b1, wg, bg, wl, bl, be
         out_pool = ctx.enter_context(tc.tile_pool(name="out", bufs=2))
         psum = ctx.enter_context(tc.psum_pool(name="psum", bufs=BANKS))
         ctx.enter_context(tc.manual_schedule())
-        loads = [("u", w1, 0)]
-        for half in range(2):
-            loads.append(("gate", wg, half))
-            loads.append(("lin", wl, half))
-        n_strips = len(loads) * STRIPS_PER_LOAD
+
+        loads = [("u", w1, 0, F, [512] * 4)]
+        loads += [("gate", wg, 0, HALF, [256] * 4), ("lin", wl, 0, HALF, [256] * 4)]
+        loads += [("gate", wg, HALF, HALF, [256] * 4), ("lin", wl, HALF, HALF, [256] * 3 + [128] * 2)]
+        strips = []
+        for s, (what, w, first, columns, widths) in enumerate(loads):
+            for n in widths:
+                strips.append((what, s, first, n))
+                first += n
+        n_strips = len(strips)
 
         def kind(i):
-            return loads[i // STRIPS_PER_LOAD][0] if 0 <= i < n_strips else "none"
+            return strips[i][0] if 0 <= i < n_strips else "none"
 
         raw_of = {}
         grouped_of = {}
@@ -73,24 +76,16 @@ def tile_llamaselfattentionblock_pb_kernel(tc, h_ffn, w1, b1, wg, bg, wl, bl, be
         turned_of = {}
 
         pieces = []
-        for s, (what, w, half) in enumerate(loads):
-            passes = w.shape[0] // K_PASS
-            width = STRIPS_PER_LOAD * WORDS // passes
+        for s, (what, w, first, total, widths) in enumerate(loads):
             group = 2 if s < 2 else 1
             columns = PIECE // PACK // group
-            for c in range(half * width, (half + 1) * width, columns):
-                for g in range(0, passes, group):
+            for c in range(first, first + total, columns):
+                for g in range(0, w.shape[0] // K_PASS, group):
                     pieces.append((s, g, group, c, columns))
 
-        def strip_columns(i):
-            s, q = divmod(i, STRIPS_PER_LOAD)
-            n = WORDS // (loads[s][1].shape[0] // K_PASS)
-            return (loads[s][2] * STRIPS_PER_LOAD + q) * n, n
-
-        def last_strip(piece):
+        def strips_of(piece):
             s, g, group, c, columns = piece
-            first, n = strip_columns(s * STRIPS_PER_LOAD)
-            return s * STRIPS_PER_LOAD + (c + columns - first) // n - 1
+            return [i for i in range(n_strips) if strips[i][1] == s and c <= strips[i][2] < c + columns]
 
         def load(piece):
             s, g, group, c, columns = piece
@@ -101,38 +96,39 @@ def tile_llamaselfattentionblock_pb_kernel(tc, h_ffn, w1, b1, wg, bg, wl, bl, be
                     out=raw[:, k * PACK : (k + 1) * PACK, :],
                     in_=w[(g + k) * K_PASS : (g + k + 1) * K_PASS, c : c + columns].rearrange("(p t) n -> p t n", t=PACK),
                 )
-                for i in range(s * STRIPS_PER_LOAD, (s + 1) * STRIPS_PER_LOAD):
-                    first, n = strip_columns(i)
-                    if c <= first < c + columns:
-                        raw_of[i, g + k] = (raw, k * PACK, first - c)
+                for i in strips_of(piece):
+                    raw_of[i, g + k] = (raw, k * PACK, strips[i][2] - c)
 
         loaded = []
 
         def load_ahead(done):
-            while len(loaded) < len(pieces) and sum(last_strip(p) >= done for p in loaded) < PIECE_BUFS:
+            while len(loaded) < len(pieces) and sum(strips_of(p)[-1] >= done for p in loaded) < PIECE_BUFS:
                 load(pieces[len(loaded)])
                 loaded.append(pieces[len(loaded)])
 
         def regroup(i):
-            first, n = strip_columns(i)
-            passes = WORDS // n
-            quarters = {"none": 2, "u": 0, "gate": 3, "lin": 2}[kind(i - FINISH_LAG)]
-            vector_passes = quarters * passes // 4
+            what, s, first, n = strips[i]
+            passes = loads[s][1].shape[0] // K_PASS
             grouped = grouped_pool.tile([P, passes, n, PACK], BF16, align_bytes=64, tag="grouped")
+            split = int(VECTOR_QUARTERS[kind(i - FINISH_LAG)] * passes * n) // 4
             for g in range(passes):
                 raw, row, col = raw_of[i, g]
-                rows = raw[:, row : row + PACK, col : col + n]
-                copy = nc.vector.tensor_copy if g < vector_passes else nc.scalar.copy
-                if kind(i) == "u":
-                    copy(
-                        out=grouped[:, g, :, :].rearrange("p (a m) t -> p a m t", a=PACK),
-                        in_=rows.rearrange("p t (m a) -> p a m t", a=PACK),
-                    )
-                else:
-                    copy(
-                        out=grouped[:, g, :, :].rearrange("p (c i) t -> p c t i", i=4),
-                        in_=rows.rearrange("p t (c i) -> p c t i", i=4),
-                    )
+                middle = min(max(split - g * n, 0), n)
+                for copy, lo, hi in ((nc.vector.tensor_copy, 0, middle), (nc.scalar.copy, middle, n)):
+                    if lo == hi:
+                        continue
+                    rows = raw[:, row : row + PACK, col + lo : col + hi]
+                    if what == "u":
+                        places = grouped[:, g, :, :].rearrange("p (a m) t -> p a m t", a=PACK)
+                        copy(
+                            out=places[:, :, lo // PACK : hi // PACK, :],
+                            in_=rows.rearrange("p t (m a) -> p a m t", a=PACK),
+                        )
+                    else:
+                        copy(
+                            out=grouped[:, g, lo:hi, :].rearrange("p (c i) t -> p c t i", i=4),
+                            in_=rows.rearrange("p t (c i) -> p c t i", i=4),
+                        )
             grouped_of[i] = grouped
             load_ahead(i + 1)
 
@@ -149,9 +145,9 @@ def tile_llamaselfattentionblock_pb_kernel(tc, h_ffn, w1, b1, wg, bg, wl, bl, be
             words_of[i] = words
             scales_of[i] = scales
 
-        def column_tile(i, j):
-            s, q = divmod(i, STRIPS_PER_LOAD)
-            return (loads[s][2] * STRIPS_PER_LOAD + q) * TILES_PER_STRIP + j
+        def column_tiles(i):
+            what, s, first, n = strips[i]
+            return range(first // P, (first + n) // P)
 
         def multiply(i):
             words, scales = words_of[i], scales_of[i]
@@ -174,7 +170,7 @@ def tile_llamaselfattentionblock_pb_kernel(tc, h_ffn, w1, b1, wg, bg, wl, bl, be
                             )
                     banks.append(u_acc)
             else:
-                for j in range(TILES_PER_STRIP):
+                for j in range(len(column_tiles(i))):
                     cols = slice(j * P, (j + 1) * P)
                     acc = psum.tile([P, TOKENS], F32, tag="bank")
                     for g in range(F_PASSES):
@@ -191,76 +187,55 @@ def tile_llamaselfattentionblock_pb_kernel(tc, h_ffn, w1, b1, wg, bg, wl, bl, be
             acc_of[i] = banks
 
         def silu(i):
-            silus = []
-            for j in range(TILES_PER_STRIP):
-                m = column_tile(i, j)
+            for acc, m in zip(acc_of[i], column_tiles(i)):
                 y = silu_pool.tile([P, TOKENS], F32)
                 nc.scalar.activation(
-                    out=y[:],
-                    in_=acc_of[i][j][:],
-                    func=ACT.Silu,
-                    bias=beta_bg_cols[:, m : m + 1],
-                    scale=beta_col[:, 0:1],
+                    out=y[:], in_=acc[:], func=ACT.Silu, bias=beta_bg_cols[:, m : m + 1], scale=beta_col[:, 0:1]
                 )
-                silus.append(y)
-            silu_of[i] = silus
+                silu_of[m] = y
 
-        def finish(i):
-            if kind(i) == "u":
-                u_grouped = u_pool.tile([P, TOKENS, PACK], BF16, align_bytes=64)
-                for b in range(BATCH):
-                    nc.vector.tensor_tensor(
-                        out=u_grouped[:, b * P : (b + 1) * P, :],
-                        in0=acc_of[i][b][:].rearrange("p t r -> p r t"),
-                        in1=b1_cols[:, i * PACK : (i + 1) * PACK].unsqueeze(1).to_broadcast([P, P, PACK]),
-                        op=ALU.add,
-                    )
-                nc.vector.quantize_mx(
-                    out=u_words[:, i, :].bitcast(FP8X4),
-                    scales=u_scales[:, i, :],
-                    in_=u_grouped[:].rearrange("p r t -> p (r t)"),
+        def add_bias(i):
+            u_grouped = u_pool.tile([P, TOKENS, PACK], BF16, align_bytes=64)
+            for b in range(BATCH):
+                nc.vector.tensor_tensor(
+                    out=u_grouped[:, b * P : (b + 1) * P, :],
+                    in0=acc_of[i][b][:].rearrange("p t r -> p r t"),
+                    in1=b1_cols[:, i * PACK : (i + 1) * PACK].unsqueeze(1).to_broadcast([P, P, PACK]),
+                    op=ALU.add,
                 )
-            elif kind(i) == "lin":
-                prods = []
-                for j in range(TILES_PER_STRIP):
-                    m = column_tile(i, j)
-                    prod = work.tile([P, TOKENS], F32, tag="prod")
-                    nc.vector.scalar_tensor_tensor(
-                        out=prod[:], in0=acc_of[i][j][:], scalar=bl_cols[:, m : m + 1],
-                        in1=silu_of[i - STRIPS_PER_LOAD][j][:], op0=ALU.add, op1=ALU.mult,
-                    )
-                    prods.append(prod)
-                prod_of[i] = prods
+            nc.vector.quantize_mx(
+                out=u_words[:, i, :].bitcast(FP8X4),
+                scales=u_scales[:, i, :],
+                in_=u_grouped[:].rearrange("p r t -> p (r t)"),
+            )
+
+        def gated(i):
+            prods = []
+            for acc, m in zip(acc_of[i], column_tiles(i)):
+                prod = work.tile([P, TOKENS], F32, tag="prod")
+                nc.vector.scalar_tensor_tensor(
+                    out=prod[:], in0=acc[:], scalar=bl_cols[:, m : m + 1], in1=silu_of[m][:], op0=ALU.add, op1=ALU.mult
+                )
+                prods.append(prod)
+            prod_of[i] = prods
 
         def turn(i):
             banks = []
-            for j in range(TILES_PER_STRIP):
+            for prod in prod_of[i]:
                 turned = psum.tile([P, BATCH, P], F32, tag="bank")
                 for b in range(BATCH):
-                    nc.tensor.transpose(
-                        out=turned[:, b, :], in_=prod_of[i][j][:, b * P : (b + 1) * P], identity=ident_f32[:]
-                    )
+                    nc.tensor.transpose(out=turned[:, b, :], in_=prod[:, b * P : (b + 1) * P], identity=ident_f32[:])
                 banks.append(turned)
             turned_of[i] = banks
 
         def store(i):
-            out_sb = out_pool.tile([P, BATCH, TILES_PER_STRIP * P], F32)
-            for j in range(TILES_PER_STRIP):
+            what, s, first, n = strips[i]
+            out_sb = out_pool.tile([P, BATCH, n], F32, tag="out")
+            for j, turned in enumerate(turned_of[i]):
                 nc.scalar.activation(
-                    out=out_sb[:, :, j * P : (j + 1) * P], in_=turned_of[i][j][:], func=ACT.Copy, scale=inv_beta_col[:, 0:1]
+                    out=out_sb[:, :, j * P : (j + 1) * P], in_=turned[:], func=ACT.Copy, scale=inv_beta_col[:, 0:1]
                 )
-            first = column_tile(i, 0) * P
-            nc.sync.dma_start(out=out_view[:, :, first : first + TILES_PER_STRIP * P], in_=out_sb[:])
-
-        tiles_g = G // P
-        bias_rows = const.tile([P, P], BF16)
-        nc.vector.memset(bias_rows[:], 0.0)
-        nc.sync.dma_start(out=bias_rows[0:tiles_g, :], in_=bg.rearrange("(m p) -> m p", p=P))
-        nc.sync.dma_start(out=bias_rows[tiles_g : 2 * tiles_g, :], in_=bl.rearrange("(m p) -> m p", p=P))
-        b1_bf16 = const.tile([P, F_PASSES, PACK], BF16)
-        nc.scalar.dma_start(out=b1_bf16[:], in_=b1.rearrange("(i p t) -> p i t", p=P, t=PACK))
-        beta_bf16 = const.tile([P, 1], BF16)
-        nc.sync.dma_start(out=beta_bf16[:], in_=beta.partition_broadcast(P))
+            nc.sync.dma_start(out=out_view[:, :, first : first + n], in_=out_sb[:])
 
         h_raw = const.tile([P, BATCH, E], BF16)
         for b in range(BATCH):
@@ -272,22 +247,34 @@ def tile_llamaselfattentionblock_pb_kernel(tc, h_ffn, w1, b1, wg, bg, wl, bl, be
         nc.vector.memset(warm[:], 0.0)
         nc.scalar.activation(out=warm[:], in_=warm[:], func=ACT.Silu)
 
-        ident_bf16 = const.tile([P, P], BF16)
-        make_identity(nc, ident_bf16[:])
+        tiles_g = G // P
+        bias_rows = const.tile([P, P], BF16)
+        nc.vector.memset(bias_rows[:], 0.0)
+        b1_bf16 = const.tile([P, F_PASSES, PACK], BF16)
+        nc.scalar.dma_start(out=b1_bf16[:], in_=b1.rearrange("(i p t) -> p i t", p=P, t=PACK))
+        beta_bf16 = const.tile([P, 1], BF16)
+        nc.scalar.dma_start(out=beta_bf16[:], in_=beta.partition_broadcast(P))
+        nc.scalar.dma_start(out=bias_rows[0:tiles_g, :], in_=bg.rearrange("(m p) -> m p", p=P))
+        nc.scalar.dma_start(out=bias_rows[tiles_g : 2 * tiles_g, :], in_=bl.rearrange("(m p) -> m p", p=P))
+
         ident_f32 = const.tile([P, P], F32)
         make_identity(nc, ident_f32[:])
+        ident_bf16 = const.tile([P, P], BF16)
+        make_identity(nc, ident_bf16[:])
 
         h_grouped = grouped_pool.tile([P, E_PASSES, TOKENS, PACK], BF16, align_bytes=64, tag="grouped")
-        for c in range(E_PASSES):
-            for b in range(BATCH):
-                h_t = psum.tile([P, PACK, P], BF16, tag="bank")
-                for t in range(PACK):
-                    k0 = c * K_PASS
+        h_pairs = h_grouped[:].rearrange("p c r t -> p c (r t)").bitcast(F32).rearrange("p c (r v) -> p c r v", v=PAIR)
+        for b in range(BATCH):
+            h_t = psum.tile([P, E_PASSES, PAIR, P], F32, tag="bank")
+            pairs = h_raw[:, b, :].bitcast(F32)
+            for c in range(E_PASSES):
+                w0 = c * K_PASS // PAIR
+                for v in range(PAIR):
                     nc.tensor.transpose(
-                        out=h_t[:, t, :], in_=h_raw[:, b, k0 + t : k0 + K_PASS : PACK], identity=ident_bf16[:]
+                        out=h_t[:, c, v, :], in_=pairs[:, w0 + v : w0 + K_PASS // PAIR : PAIR], identity=ident_f32[:]
                     )
-                copy = nc.vector.tensor_copy if b % 2 == 0 else nc.scalar.copy
-                copy(out=h_grouped[:, c, b * P : (b + 1) * P, :], in_=h_t[:].rearrange("p t r -> p r t"))
+            copy = nc.vector.tensor_copy if b % 2 == 0 else nc.scalar.copy
+            copy(out=h_pairs[:, :, b * P : (b + 1) * P, :], in_=h_t[:].rearrange("p c v r -> p c r v"))
         h_words = const.tile([P, E_PASSES, TOKENS], U32, align_bytes=64)
         h_scales = const.tile([P, E_PASSES, TOKENS], U8, align_bytes=64)
         nc.vector.quantize_mx(
@@ -327,17 +314,19 @@ def tile_llamaselfattentionblock_pb_kernel(tc, h_ffn, w1, b1, wg, bg, wl, bl, be
         u_words = const.tile([P, F_PASSES, TOKENS], U32, align_bytes=64)
         u_scales = const.tile([P, F_PASSES, TOKENS], U8, align_bytes=64)
 
-        for step in range(n_strips + STORE_LAG):
+        for step in range(n_strips + TURN_LAG):
             if kind(step - TURN_LAG) == "lin":
                 turn(step - TURN_LAG)
-            if kind(step - SILU_LAG) == "gate":
-                silu(step - SILU_LAG)
+            if kind(step - FINISH_LAG) == "gate":
+                silu(step - FINISH_LAG)
             if kind(step) != "none":
                 regroup(step)
-            if kind(step - STORE_LAG) == "lin":
-                store(step - STORE_LAG)
-            if kind(step - FINISH_LAG) != "none":
-                finish(step - FINISH_LAG)
+            if kind(step - TURN_LAG) == "lin":
+                store(step - TURN_LAG)
+            if kind(step - FINISH_LAG) == "u":
+                add_bias(step - FINISH_LAG)
+            if kind(step - FINISH_LAG) == "lin":
+                gated(step - FINISH_LAG)
             if kind(step - QUANTISE_LAG) != "none":
                 quantise(step - QUANTISE_LAG)
             if kind(step - MULTIPLY_LAG) != "none":

@@ -25,6 +25,7 @@ E_PASSES = E // K_PASS
 F_PASSES = F // K_PASS
 
 HALF = G // 2
+RUN = 8
 PIECE = 4096
 PIECE_BUFS = 13
 BANKS = 8
@@ -126,8 +127,8 @@ def tile_llamaselfattentionblock_pb_kernel(tc, h_ffn, w1, b1, wg, bg, wl, bl, be
                         )
                     else:
                         copy(
-                            out=grouped[:, g, lo:hi, :].rearrange("p (c i) t -> p c t i", i=4),
-                            in_=rows.rearrange("p t (c i) -> p c t i", i=4),
+                            out=grouped[:, g, lo:hi, :].rearrange("p (c i) t -> p c t i", i=RUN),
+                            in_=rows.rearrange("p t (c i) -> p c t i", i=RUN),
                         )
             grouped_of[i] = grouped
             load_ahead(i + 1)
@@ -317,10 +318,10 @@ def tile_llamaselfattentionblock_pb_kernel(tc, h_ffn, w1, b1, wg, bg, wl, bl, be
         for step in range(n_strips + TURN_LAG):
             if kind(step - TURN_LAG) == "lin":
                 turn(step - TURN_LAG)
-            if kind(step - FINISH_LAG) == "gate":
-                silu(step - FINISH_LAG)
             if kind(step) != "none":
                 regroup(step)
+            if kind(step - FINISH_LAG) == "gate":
+                silu(step - FINISH_LAG)
             if kind(step - TURN_LAG) == "lin":
                 store(step - TURN_LAG)
             if kind(step - FINISH_LAG) == "u":

@@ -35,7 +35,8 @@ MULTIPLY_LAG = 2
 FINISH_LAG = 3
 TURN_LAG = 4
 
-VECTOR_QUARTERS = {"none": 2.0, "u": 0.5, "gate": 2.5, "lin": 2.0}
+VECTOR_QUARTERS = {"none": 2.0, "u": 0.0, "gate": 2.25, "lin": 1.75}
+GPSIMD_QUARTERS = {"none": 0.0, "u": 1.0, "gate": 0.0, "lin": 0.5}
 
 FLOPS = 2 * TOKENS * E * F + 2 * 2 * TOKENS * F * G
 
@@ -68,6 +69,7 @@ def tile_llamaselfattentionblock_pb_kernel(tc, h_ffn, w1, b1, wg, bg, wl, bl, be
             return strips[i][0] if 0 <= i < n_strips else "none"
 
         raw_of = {}
+        left_of = {}
         grouped_of = {}
         words_of = {}
         scales_of = {}
@@ -111,27 +113,40 @@ def tile_llamaselfattentionblock_pb_kernel(tc, h_ffn, w1, b1, wg, bg, wl, bl, be
             what, s, first, n = strips[i]
             passes = loads[s][1].shape[0] // K_PASS
             grouped = grouped_pool.tile([P, passes, n, PACK], BF16, align_bytes=64, tag="grouped")
-            split = int(VECTOR_QUARTERS[kind(i - FINISH_LAG)] * passes * n) // 4
-            for g in range(passes):
-                raw, row, col = raw_of[i, g]
-                middle = min(max(split - g * n, 0), n)
-                for copy, lo, hi in ((nc.vector.tensor_copy, 0, middle), (nc.scalar.copy, middle, n)):
-                    if lo == hi:
-                        continue
-                    rows = raw[:, row : row + PACK, col + lo : col + hi]
-                    if what == "u":
-                        places = grouped[:, g, :, :].rearrange("p (a m) t -> p a m t", a=PACK)
-                        copy(
-                            out=places[:, :, lo // PACK : hi // PACK, :],
-                            in_=rows.rearrange("p t (m a) -> p a m t", a=PACK),
-                        )
-                    else:
-                        copy(
-                            out=grouped[:, g, lo:hi, :].rearrange("p (c i) t -> p c t i", i=RUN),
-                            in_=rows.rearrange("p t (c i) -> p c t i", i=RUN),
-                        )
+            vector_end = int(VECTOR_QUARTERS[kind(i - FINISH_LAG)] * passes * n) // 4
+            scalar_end = passes * n - int(GPSIMD_QUARTERS[kind(i - FINISH_LAG)] * passes * n) // 4
             grouped_of[i] = grouped
-            load_ahead(i + 1)
+            for g in range(passes):
+                first_scalar = min(max(vector_end - g * n, 0), n)
+                end_scalar = min(scalar_end - g * n, n)
+                for copy, lo, hi in ((nc.vector.tensor_copy, 0, first_scalar), (nc.scalar.copy, first_scalar, end_scalar)):
+                    if lo < hi:
+                        target, source = regrouping(i, g, lo, hi)
+                        copy(out=target, in_=source)
+            left_of[i] = passes - 1, scalar_end - (passes - 1) * n, n
+
+        def regrouping(i, g, lo, hi):
+            raw, row, col = raw_of[i, g]
+            rows = raw[:, row : row + PACK, col + lo : col + hi]
+            places = grouped_of[i][:, g, :, :]
+            if kind(i) == "u":
+                places = places.rearrange("p (a m) t -> p a m t", a=PACK)[:, :, lo // PACK : hi // PACK, :]
+                return places, rows.rearrange("p t (m a) -> p a m t", a=PACK)
+            return (
+                places[:, lo:hi, :].rearrange("p (c i) t -> p c t i", i=RUN),
+                rows.rearrange("p t (c i) -> p c t i", i=RUN),
+            )
+
+        def regroup_on_gpsimd(i):
+            g, lo, hi = left_of[i]
+            if lo == hi:
+                return
+            one = work.tile([P, 1], F32, tag="one")
+            nc.vector.memset(one[:], 1.0)
+            target, source = regrouping(i, g, lo, hi)
+            nc.gpsimd.tensor_scalar(
+                out=target, in0=source, scalar1=one[:, 0:1], scalar2=0.0, op0=ALU.mult, op1=ALU.add
+            )
 
         def quantise(i):
             grouped = grouped_of[i]
@@ -324,6 +339,9 @@ def tile_llamaselfattentionblock_pb_kernel(tc, h_ffn, w1, b1, wg, bg, wl, bl, be
                 silu(step - FINISH_LAG)
             if kind(step - TURN_LAG) == "lin":
                 store(step - TURN_LAG)
+            if kind(step) != "none":
+                regroup_on_gpsimd(step)
+                load_ahead(step + 1)
             if kind(step - FINISH_LAG) == "u":
                 add_bias(step - FINISH_LAG)
             if kind(step - FINISH_LAG) == "lin":

@@ -125,7 +125,7 @@ def tile_llamaselfattentionblock_pb_kernel(tc, h_ffn, w1, b1, wg, bg, wl, bl, be
                         copy(out=target, in_=source)
             left_of[i] = passes - 1, scalar_end - (passes - 1) * n, n
 
-        def regrouping(i, g, lo, hi):
+        def regrouping(i, g, lo, hi, run=RUN):
             raw, row, col = raw_of[i, g]
             rows = raw[:, row : row + PACK, col + lo : col + hi]
             places = grouped_of[i][:, g, :, :]
@@ -133,8 +133,8 @@ def tile_llamaselfattentionblock_pb_kernel(tc, h_ffn, w1, b1, wg, bg, wl, bl, be
                 places = places.rearrange("p (a m) t -> p a m t", a=PACK)[:, :, lo // PACK : hi // PACK, :]
                 return places, rows.rearrange("p t (m a) -> p a m t", a=PACK)
             return (
-                places[:, lo:hi, :].rearrange("p (c i) t -> p c t i", i=RUN),
-                rows.rearrange("p t (c i) -> p c t i", i=RUN),
+                places[:, lo:hi, :].rearrange("p (c i) t -> p c t i", i=run),
+                rows.rearrange("p t (c i) -> p c t i", i=run),
             )
 
         def regroup_on_gpsimd(i):
@@ -143,7 +143,7 @@ def tile_llamaselfattentionblock_pb_kernel(tc, h_ffn, w1, b1, wg, bg, wl, bl, be
                 return
             one = work.tile([P, 1], F32, tag="one")
             nc.vector.memset(one[:], 1.0)
-            target, source = regrouping(i, g, lo, hi)
+            target, source = regrouping(i, g, lo, hi, run=1)
             nc.gpsimd.tensor_scalar(
                 out=target, in0=source, scalar1=one[:, 0:1], scalar2=0.0, op0=ALU.mult, op1=ALU.add
             )

@@ -51,13 +51,13 @@ def tile_llamaselfattentionblock_pb_kernel(tc, h_ffn, w1, b1, wg, bg, wl, bl, be
         u_pool = ctx.enter_context(tc.tile_pool(name="u", bufs=2))
         silu_pool = ctx.enter_context(tc.tile_pool(name="silu", bufs=12))
         work = ctx.enter_context(tc.tile_pool(name="work", bufs=4))
-        out_pool = ctx.enter_context(tc.tile_pool(name="out", bufs=2))
+        out_pool = ctx.enter_context(tc.tile_pool(name="out", bufs=4))
         psum = ctx.enter_context(tc.psum_pool(name="psum", bufs=BANKS))
         ctx.enter_context(tc.manual_schedule())
 
         loads = [("u", w1, 0, F, [512] * 4)]
         loads += [("gate", wg, 0, HALF, [256] * 4), ("lin", wl, 0, HALF, [256] * 4)]
-        loads += [("gate", wg, HALF, HALF, [256] * 4), ("lin", wl, HALF, HALF, [256] * 3 + [128] * 2)]
+        loads += [("gate", wg, HALF, HALF, [256] * 4), ("lin", wl, HALF, HALF, [256] * 2 + [128] * 4)]
         strips = []
         for s, (what, w, first, columns, widths) in enumerate(loads):
             for n in widths:
@@ -302,35 +302,36 @@ def tile_llamaselfattentionblock_pb_kernel(tc, h_ffn, w1, b1, wg, bg, wl, bl, be
         bias_t = psum.tile([P, P], BF16, tag="bank")
         nc.tensor.transpose(out=bias_t[:], in_=bias_rows[:], identity=ident_bf16[:])
         bias_cols = const.tile([P, 2 * tiles_g], F32)
-        nc.vector.tensor_copy(out=bias_cols[:], in_=bias_t[:, 0 : 2 * tiles_g])
+        nc.scalar.copy(out=bias_cols[:], in_=bias_t[:, 0 : 2 * tiles_g])
         b1_cols = const.tile([P, F_PASSES * PACK], F32)
-        nc.vector.tensor_copy(out=b1_cols[:], in_=b1_bf16[:].rearrange("p i t -> p (i t)"))
+        nc.gpsimd.tensor_copy(out=b1_cols[:], in_=b1_bf16[:].rearrange("p i t -> p (i t)"))
         bg_cols = bias_cols[:, 0:tiles_g]
         bl_cols = bias_cols[:, tiles_g : 2 * tiles_g]
         beta_f32 = const.tile([P, 1], F32)
-        nc.vector.tensor_copy(out=beta_f32[:], in_=beta_bf16[:])
+        nc.gpsimd.tensor_copy(out=beta_f32[:], in_=beta_bf16[:])
         beta_sign = const.tile([P, 1], F32)
-        nc.vector.tensor_scalar(out=beta_sign[:], in0=beta_f32[:], scalar1=0.0, scalar2=2.0, op0=ALU.is_ge, op1=ALU.mult)
+        nc.gpsimd.tensor_scalar(out=beta_sign[:], in0=beta_f32[:], scalar1=0.0, scalar2=2.0, op0=ALU.is_ge, op1=ALU.mult)
+        nc.gpsimd.tensor_scalar(out=beta_sign[:], in0=beta_sign[:], scalar1=1.0, scalar2=-1.0, op0=ALU.mult, op1=ALU.add)
         beta_abs = const.tile([P, 1], F32)
-        nc.vector.scalar_tensor_tensor(
-            out=beta_abs[:], in0=beta_f32[:], scalar=-1.0, in1=beta_f32[:], op0=ALU.mult, op1=ALU.max
-        )
-        nc.vector.tensor_scalar(
+        nc.gpsimd.tensor_tensor(out=beta_abs[:], in0=beta_f32[:], in1=beta_sign[:], op=ALU.mult)
+        nc.gpsimd.tensor_scalar(
             out=beta_abs[:], in0=beta_abs[:], scalar1=2.0**-30, scalar2=2.0**64, op0=ALU.max, op1=ALU.min
         )
         beta_col = const.tile([P, 1], F32)
-        nc.vector.scalar_tensor_tensor(
-            out=beta_col[:], in0=beta_sign[:], scalar=-1.0, in1=beta_abs[:], op0=ALU.add, op1=ALU.mult
-        )
+        nc.gpsimd.tensor_tensor(out=beta_col[:], in0=beta_abs[:], in1=beta_sign[:], op=ALU.mult)
         inv_beta_col = const.tile([P, 1], F32)
-        nc.vector.reciprocal(out=inv_beta_col[:], in_=beta_col[:])
         beta_bg_cols = const.tile([P, tiles_g], F32)
-        nc.vector.tensor_scalar_mul(out=beta_bg_cols[:], in0=bg_cols, scalar1=beta_col[:, 0:1])
+        nc.gpsimd.tensor_scalar(
+            out=beta_bg_cols[:], in0=bg_cols, scalar1=beta_col[:, 0:1], scalar2=0.0, op0=ALU.mult, op1=ALU.add
+        )
 
         u_words = const.tile([P, F_PASSES, TOKENS], U32, align_bytes=64)
         u_scales = const.tile([P, F_PASSES, TOKENS], U8, align_bytes=64)
 
+        first_lin = min(i for i in range(n_strips) if kind(i) == "lin")
         for step in range(n_strips + TURN_LAG):
+            if step == first_lin:
+                nc.vector.reciprocal(out=inv_beta_col[:], in_=beta_col[:])
             if kind(step - TURN_LAG) == "lin":
                 turn(step - TURN_LAG)
             if kind(step) != "none":

@@ -27,15 +27,16 @@ F_PASSES = F // K_PASS
 HALF = G // 2
 RUN = 8
 PIECE = 4096
-PIECE_BUFS = 13
+PIECE_BUFS = 12
 BANKS = 8
 
 QUANTISE_LAG = 1
 MULTIPLY_LAG = 2
 FINISH_LAG = 3
+SILU_LAG = 4
 TURN_LAG = 4
 
-VECTOR_QUARTERS = {"none": 2.0, "u": 0.0, "gate": 2.25, "lin": 1.75}
+VECTOR_QUARTERS = {"none": 2.0, "u": 0.0, "gate": 2.125, "lin": 1.75}
 GPSIMD_QUARTERS = {"none": 0.0, "u": 1.0, "gate": 0.0, "lin": 0.5}
 
 FLOPS = 2 * TOKENS * E * F + 2 * 2 * TOKENS * F * G
@@ -46,7 +47,7 @@ def tile_llamaselfattentionblock_pb_kernel(tc, h_ffn, w1, b1, wg, bg, wl, bl, be
     with ExitStack() as ctx:
         const = ctx.enter_context(tc.tile_pool(name="const", bufs=1))
         raw_pool = ctx.enter_context(tc.tile_pool(name="raw", bufs=PIECE_BUFS))
-        grouped_pool = ctx.enter_context(tc.tile_pool(name="grouped", bufs=3))
+        grouped_pool = ctx.enter_context(tc.tile_pool(name="grouped", bufs=4))
         strip_pool = ctx.enter_context(tc.tile_pool(name="strip", bufs=4))
         u_pool = ctx.enter_context(tc.tile_pool(name="u", bufs=2))
         silu_pool = ctx.enter_context(tc.tile_pool(name="silu", bufs=12))
@@ -73,6 +74,7 @@ def tile_llamaselfattentionblock_pb_kernel(tc, h_ffn, w1, b1, wg, bg, wl, bl, be
         grouped_of = {}
         words_of = {}
         scales_of = {}
+        u_grouped_of = {}
         acc_of = {}
         silu_of = {}
         prod_of = {}
@@ -80,7 +82,7 @@ def tile_llamaselfattentionblock_pb_kernel(tc, h_ffn, w1, b1, wg, bg, wl, bl, be
 
         pieces = []
         for s, (what, w, first, total, widths) in enumerate(loads):
-            group = 2 if s < 2 else 1
+            group = 2 if s < 3 else 1
             columns = PIECE // PACK // group
             for c in range(first, first + total, columns):
                 for g in range(0, w.shape[0] // K_PASS, group):
@@ -165,6 +167,11 @@ def tile_llamaselfattentionblock_pb_kernel(tc, h_ffn, w1, b1, wg, bg, wl, bl, be
             what, s, first, n = strips[i]
             return range(first // P, (first + n) // P)
 
+        def parts_of(i):
+            halves = 2 if i == n_strips - 1 else 1
+            size = BATCH // halves
+            return [(m, h * size, (h + 1) * size) for m in column_tiles(i) for h in range(halves)]
+
         def multiply(i):
             words, scales = words_of[i], scales_of[i]
             banks = []
@@ -186,16 +193,17 @@ def tile_llamaselfattentionblock_pb_kernel(tc, h_ffn, w1, b1, wg, bg, wl, bl, be
                             )
                     banks.append(u_acc)
             else:
-                for j in range(len(column_tiles(i))):
-                    cols = slice(j * P, (j + 1) * P)
-                    acc = psum.tile([P, TOKENS], F32, tag="bank")
+                for m, first_b, end_b in parts_of(i):
+                    cols = slice(m * P - strips[i][2], (m + 1) * P - strips[i][2])
+                    tokens = slice(first_b * P, end_b * P)
+                    acc = psum.tile([P, (end_b - first_b) * P], F32, tag="bank")
                     for g in range(F_PASSES):
                         nc.tensor.matmul_mx(
                             out=acc[:],
                             lhsT=words[:, g, cols].bitcast(FP8X4),
                             lhsT_scale=scales[:, g, cols],
-                            rhs=u_words[:, g, :].bitcast(FP8X4),
-                            rhs_scale=u_scales[:, g, :],
+                            rhs=u_words[:, g, tokens].bitcast(FP8X4),
+                            rhs_scale=u_scales[:, g, tokens],
                             start=(g == 0),
                             stop=(g == F_PASSES - 1),
                         )
@@ -219,27 +227,31 @@ def tile_llamaselfattentionblock_pb_kernel(tc, h_ffn, w1, b1, wg, bg, wl, bl, be
                     in1=b1_cols[:, i * PACK : (i + 1) * PACK].unsqueeze(1).to_broadcast([P, P, PACK]),
                     op=ALU.add,
                 )
+            u_grouped_of[i] = u_grouped
+
+        def quantise_u(i):
             nc.vector.quantize_mx(
                 out=u_words[:, i, :].bitcast(FP8X4),
                 scales=u_scales[:, i, :],
-                in_=u_grouped[:].rearrange("p r t -> p (r t)"),
+                in_=u_grouped_of[i][:].rearrange("p r t -> p (r t)"),
             )
 
         def gated(i):
             prods = []
-            for acc, m in zip(acc_of[i], column_tiles(i)):
-                prod = work.tile([P, TOKENS], F32, tag="prod")
+            for acc, (m, first_b, end_b) in zip(acc_of[i], parts_of(i)):
+                prod = work.tile([P, (end_b - first_b) * P], F32, tag="prod")
                 nc.vector.scalar_tensor_tensor(
-                    out=prod[:], in0=acc[:], scalar=bl_cols[:, m : m + 1], in1=silu_of[m][:], op0=ALU.add, op1=ALU.mult
+                    out=prod[:], in0=acc[:], scalar=bl_cols[:, m : m + 1],
+                    in1=silu_of[m][:, first_b * P : end_b * P], op0=ALU.add, op1=ALU.mult,
                 )
                 prods.append(prod)
             prod_of[i] = prods
 
         def turn(i):
             banks = []
-            for prod in prod_of[i]:
-                turned = psum.tile([P, BATCH, P], F32, tag="bank")
-                for b in range(BATCH):
+            for prod, (m, first_b, end_b) in zip(prod_of[i], parts_of(i)):
+                turned = psum.tile([P, end_b - first_b, P], F32, tag="bank")
+                for b in range(end_b - first_b):
                     nc.tensor.transpose(out=turned[:, b, :], in_=prod[:, b * P : (b + 1) * P], identity=ident_f32[:])
                 banks.append(turned)
             turned_of[i] = banks
@@ -247,11 +259,16 @@ def tile_llamaselfattentionblock_pb_kernel(tc, h_ffn, w1, b1, wg, bg, wl, bl, be
         def store(i):
             what, s, first, n = strips[i]
             out_sb = out_pool.tile([P, BATCH, n], F32, tag="out")
-            for j, turned in enumerate(turned_of[i]):
-                nc.scalar.activation(
-                    out=out_sb[:, :, j * P : (j + 1) * P], in_=turned[:], func=ACT.Copy, scale=inv_beta_col[:, 0:1]
-                )
-            nc.sync.dma_start(out=out_view[:, :, first : first + n], in_=out_sb[:])
+            stores = set()
+            for turned, (m, first_b, end_b) in zip(turned_of[i], parts_of(i)):
+                target = out_sb[:, first_b:end_b, m * P - first : (m + 1) * P - first]
+                if first_b == 0:
+                    nc.scalar.activation(out=target, in_=turned[:], func=ACT.Copy, scale=inv_beta_col[:, 0:1])
+                else:
+                    nc.vector.tensor_scalar_mul(out=target, in0=turned[:], scalar1=inv_beta_col[:, 0:1])
+                stores.add((first_b, end_b))
+            for first_b, end_b in sorted(stores):
+                nc.sync.dma_start(out=out_view[:, first_b:end_b, first : first + n], in_=out_sb[:, first_b:end_b, :])
 
         h_raw = const.tile([P, BATCH, E], BF16)
         for b in range(BATCH):
@@ -281,16 +298,16 @@ def tile_llamaselfattentionblock_pb_kernel(tc, h_ffn, w1, b1, wg, bg, wl, bl, be
         h_grouped = grouped_pool.tile([P, E_PASSES, TOKENS, PACK], BF16, align_bytes=64, tag="grouped")
         h_pairs = h_grouped[:].rearrange("p c r t -> p c (r t)").bitcast(F32).rearrange("p c (r v) -> p c r v", v=PAIR)
         for b in range(BATCH):
-            h_t = psum.tile([P, E_PASSES, PAIR, P], F32, tag="bank")
             pairs = h_raw[:, b, :].bitcast(F32)
             for c in range(E_PASSES):
+                h_t = psum.tile([P, PAIR, P], F32, tag="bank")
                 w0 = c * K_PASS // PAIR
                 for v in range(PAIR):
                     nc.tensor.transpose(
-                        out=h_t[:, c, v, :], in_=pairs[:, w0 + v : w0 + K_PASS // PAIR : PAIR], identity=ident_f32[:]
+                        out=h_t[:, v, :], in_=pairs[:, w0 + v : w0 + K_PASS // PAIR : PAIR], identity=ident_f32[:]
                     )
-            copy = nc.vector.tensor_copy if b % 2 == 0 else nc.scalar.copy
-            copy(out=h_pairs[:, :, b * P : (b + 1) * P, :], in_=h_t[:].rearrange("p c v r -> p c r v"))
+                copy = nc.vector.tensor_copy if c == 0 else nc.scalar.copy
+                copy(out=h_pairs[:, c, b * P : (b + 1) * P, :], in_=h_t[:].rearrange("p v r -> p r v"))
         h_words = const.tile([P, E_PASSES, TOKENS], U32, align_bytes=64)
         h_scales = const.tile([P, E_PASSES, TOKENS], U8, align_bytes=64)
         nc.vector.quantize_mx(
@@ -336,8 +353,8 @@ def tile_llamaselfattentionblock_pb_kernel(tc, h_ffn, w1, b1, wg, bg, wl, bl, be
                 turn(step - TURN_LAG)
             if kind(step) != "none":
                 regroup(step)
-            if kind(step - FINISH_LAG) == "gate":
-                silu(step - FINISH_LAG)
+            if kind(step - SILU_LAG) == "gate":
+                silu(step - SILU_LAG)
             if kind(step - TURN_LAG) == "lin":
                 store(step - TURN_LAG)
             if kind(step) != "none":
@@ -349,5 +366,7 @@ def tile_llamaselfattentionblock_pb_kernel(tc, h_ffn, w1, b1, wg, bg, wl, bl, be
                 gated(step - FINISH_LAG)
             if kind(step - QUANTISE_LAG) != "none":
                 quantise(step - QUANTISE_LAG)
+            if kind(step - FINISH_LAG) == "u":
+                quantise_u(step - FINISH_LAG)
             if kind(step - MULTIPLY_LAG) != "none":
                 multiply(step - MULTIPLY_LAG)

from contextlib import ExitStack

import concourse.mybir as mybir
from concourse.masks import make_identity

BF16 = mybir.dt.bfloat16
F32 = mybir.dt.float32
U32 = mybir.dt.uint32
U8 = mybir.dt.uint8
FP8X4 = mybir.dt.float8_e4m3fn_x4
ACT = mybir.ActivationFunctionType
ALU = mybir.AluOpType

P = 128
PACK = 4
PAIR = 2
K_PASS = P * PACK

BATCH = 4
TOKENS = BATCH * P
E = 1024
F = 2048
G = 2048
E_PASSES = E // K_PASS
F_PASSES = F // K_PASS

HALF = G // 2
RUN = 8
PIECE = 4096
PIECE_BUFS = 12
BANKS = 8

QUANTISE_LAG = 1
MULTIPLY_LAG = 2
FINISH_LAG = 3
SILU_LAG = 4
TURN_LAG = 4

VECTOR_QUARTERS = {"none": 2.0, "u": 0.0, "gate": 2.125, "lin": 1.75}
GPSIMD_QUARTERS = {"none": 0.0, "u": 1.0, "gate": 0.0, "lin": 0.5}

FLOPS = 2 * TOKENS * E * F + 2 * 2 * TOKENS * F * G


def tile_llamaselfattentionblock_pb_kernel(tc, h_ffn, w1, b1, wg, bg, wl, bl, beta, out):
    nc = tc.nc
    with ExitStack() as ctx:
        const = ctx.enter_context(tc.tile_pool(name="const", bufs=1))
        raw_pool = ctx.enter_context(tc.tile_pool(name="raw", bufs=PIECE_BUFS))
        grouped_pool = ctx.enter_context(tc.tile_pool(name="grouped", bufs=4))
        strip_pool = ctx.enter_context(tc.tile_pool(name="strip", bufs=4))
        u_pool = ctx.enter_context(tc.tile_pool(name="u", bufs=2))
        silu_pool = ctx.enter_context(tc.tile_pool(name="silu", bufs=12))
        work = ctx.enter_context(tc.tile_pool(name="work", bufs=4))
        out_pool = ctx.enter_context(tc.tile_pool(name="out", bufs=4))
        psum = ctx.enter_context(tc.psum_pool(name="psum", bufs=BANKS))
        ctx.enter_context(tc.manual_schedule())

        loads = [("u", w1, 0, F, [512] * 4)]
        loads += [("gate", wg, 0, HALF, [256] * 4), ("lin", wl, 0, HALF, [256] * 4)]
        loads += [("gate", wg, HALF, HALF, [256] * 4), ("lin", wl, HALF, HALF, [256] * 2 + [128] * 4)]
        strips = []
        for s, (what, w, first, columns, widths) in enumerate(loads):
            for n in widths:
                strips.append((what, s, first, n))
                first += n
        n_strips = len(strips)

        def kind(i):
            return strips[i][0] if 0 <= i < n_strips else "none"

        raw_of = {}
        left_of = {}
        grouped_of = {}
        words_of = {}
        scales_of = {}
        u_grouped_of = {}
        acc_of = {}
        silu_of = {}
        prod_of = {}
        turned_of = {}

        pieces = []
        for s, (what, w, first, total, widths) in enumerate(loads):
            group = 2 if s < 3 else 1
            columns = PIECE // PACK // group
            for c in range(first, first + total, columns):
                for g in range(0, w.shape[0] // K_PASS, group):
                    pieces.append((s, g, group, c, columns))

        def strips_of(piece):
            s, g, group, c, columns = piece
            return [i for i in range(n_strips) if strips[i][1] == s and c <= strips[i][2] < c + columns]

        def load(piece):
            s, g, group, c, columns = piece
            w = loads[s][1]
            raw = raw_pool.tile([P, group * PACK, columns], BF16, tag="raw")
            for k in range(group):
                nc.sync.dma_start(
                    out=raw[:, k * PACK : (k + 1) * PACK, :],
                    in_=w[(g + k) * K_PASS : (g + k + 1) * K_PASS, c : c + columns].rearrange("(p t) n -> p t n", t=PACK),
                )
                for i in strips_of(piece):
                    raw_of[i, g + k] = (raw, k * PACK, strips[i][2] - c)

        loaded = []

        def load_ahead(done):
            while len(loaded) < len(pieces) and sum(strips_of(p)[-1] >= done for p in loaded) < PIECE_BUFS:
                load(pieces[len(loaded)])
                loaded.append(pieces[len(loaded)])

        def regroup(i):
            what, s, first, n = strips[i]
            passes = loads[s][1].shape[0] // K_PASS
            grouped = grouped_pool.tile([P, passes, n, PACK], BF16, align_bytes=64, tag="grouped")
            vector_end = int(VECTOR_QUARTERS[kind(i - FINISH_LAG)] * passes * n) // 4
            scalar_end = passes * n - int(GPSIMD_QUARTERS[kind(i - FINISH_LAG)] * passes * n) // 4
            grouped_of[i] = grouped
            for g in range(passes):
                first_scalar = min(max(vector_end - g * n, 0), n)
                end_scalar = min(scalar_end - g * n, n)
                for copy, lo, hi in ((nc.vector.tensor_copy, 0, first_scalar), (nc.scalar.copy, first_scalar, end_scalar)):
                    if lo < hi:
                        target, source = regrouping(i, g, lo, hi)
                        copy(out=target, in_=source)
            left_of[i] = passes - 1, scalar_end - (passes - 1) * n, n

        def regrouping(i, g, lo, hi, run=RUN):
            raw, row, col = raw_of[i, g]
            rows = raw[:, row : row + PACK, col + lo : col + hi]
            places = grouped_of[i][:, g, :, :]
            if kind(i) == "u":
                places = places.rearrange("p (a m) t -> p a m t", a=PACK)[:, :, lo // PACK : hi // PACK, :]
                return places, rows.rearrange("p t (m a) -> p a m t", a=PACK)
            return (
                places[:, lo:hi, :].rearrange("p (c i) t -> p c t i", i=run),
                rows.rearrange("p t (c i) -> p c t i", i=run),
            )

        def regroup_on_gpsimd(i):
            g, lo, hi = left_of[i]
            if lo == hi:
                return
            one = work.tile([P, 1], F32, tag="one")
            nc.vector.memset(one[:], 1.0)
            target, source = regrouping(i, g, lo, hi, run=1)
            nc.gpsimd.tensor_scalar(
                out=target, in0=source, scalar1=one[:, 0:1], scalar2=0.0, op0=ALU.mult, op1=ALU.add
            )

        def quantise(i):
            grouped = grouped_of[i]
            passes, n = grouped.shape[1], grouped.shape[2]
            words = strip_pool.tile([P, passes, n], U32, align_bytes=64, tag="words")
            scales = strip_pool.tile([P, passes, n], U8, align_bytes=64, tag="scales")
            nc.vector.quantize_mx(
                out=words[:].rearrange("p g n -> p (g n)").bitcast(FP8X4),
                scales=scales[:].rearrange("p g n -> p (g n)"),
                in_=grouped[:].rearrange("p g n t -> p (g n t)"),
            )
            words_of[i] = words
            scales_of[i] = scales

        def column_tiles(i):
            what, s, first, n = strips[i]
            return range(first // P, (first + n) // P)

        def parts_of(i):
            halves = 2 if i == n_strips - 1 else 1
            size = BATCH // halves
            return [(m, h * size, (h + 1) * size) for m in column_tiles(i) for h in range(halves)]

        def multiply(i):
            words, scales = words_of[i], scales_of[i]
            banks = []
            if kind(i) == "u":
                for b in range(BATCH):
                    tokens = slice(b * P, (b + 1) * P)
                    u_acc = psum.tile([P, PACK, P], F32, tag="bank")
                    for t in range(PACK):
                        features = slice(t * P, (t + 1) * P)
                        for c in range(E_PASSES):
                            nc.tensor.matmul_mx(
                                out=u_acc[:, t, :],
                                lhsT=words[:, c, features].bitcast(FP8X4),
                                lhsT_scale=scales[:, c, features],
                                rhs=h_words[:, c, tokens].bitcast(FP8X4),
                                rhs_scale=h_scales[:, c, tokens],
                                start=(c == 0),
                                stop=(c == E_PASSES - 1),
                            )
                    banks.append(u_acc)
            else:
                for m, first_b, end_b in parts_of(i):
                    cols = slice(m * P - strips[i][2], (m + 1) * P - strips[i][2])
                    tokens = slice(first_b * P, end_b * P)
                    acc = psum.tile([P, (end_b - first_b) * P], F32, tag="bank")
                    for g in range(F_PASSES):
                        nc.tensor.matmul_mx(
                            out=acc[:],
                            lhsT=words[:, g, cols].bitcast(FP8X4),
                            lhsT_scale=scales[:, g, cols],
                            rhs=u_words[:, g, tokens].bitcast(FP8X4),
                            rhs_scale=u_scales[:, g, tokens],
                            start=(g == 0),
                            stop=(g == F_PASSES - 1),
                        )
                    banks.append(acc)
            acc_of[i] = banks

        def silu(i):
            for acc, m in zip(acc_of[i], column_tiles(i)):
                y = silu_pool.tile([P, TOKENS], F32)
                nc.scalar.activation(
                    out=y[:], in_=acc[:], func=ACT.Silu, bias=beta_bg_cols[:, m : m + 1], scale=beta_col[:, 0:1]
                )
                silu_of[m] = y

        def add_bias(i):
            u_grouped = u_pool.tile([P, TOKENS, PACK], BF16, align_bytes=64)
            for b in range(BATCH):
                nc.vector.tensor_tensor(
                    out=u_grouped[:, b * P : (b + 1) * P, :],
                    in0=acc_of[i][b][:].rearrange("p t r -> p r t"),
                    in1=b1_cols[:, i * PACK : (i + 1) * PACK].unsqueeze(1).to_broadcast([P, P, PACK]),
                    op=ALU.add,
                )
            u_grouped_of[i] = u_grouped

        def quantise_u(i):
            nc.vector.quantize_mx(
                out=u_words[:, i, :].bitcast(FP8X4),
                scales=u_scales[:, i, :],
                in_=u_grouped_of[i][:].rearrange("p r t -> p (r t)"),
            )

        def gated(i):
            prods = []
            for acc, (m, first_b, end_b) in zip(acc_of[i], parts_of(i)):
                prod = work.tile([P, (end_b - first_b) * P], F32, tag="prod")
                nc.vector.scalar_tensor_tensor(
                    out=prod[:], in0=acc[:], scalar=bl_cols[:, m : m + 1],
                    in1=silu_of[m][:, first_b * P : end_b * P], op0=ALU.add, op1=ALU.mult,
                )
                prods.append(prod)
            prod_of[i] = prods

        def turn(i):
            banks = []
            for prod, (m, first_b, end_b) in zip(prod_of[i], parts_of(i)):
                turned = psum.tile([P, end_b - first_b, P], F32, tag="bank")
                for b in range(end_b - first_b):
                    nc.tensor.transpose(out=turned[:, b, :], in_=prod[:, b * P : (b + 1) * P], identity=ident_f32[:])
                banks.append(turned)
            turned_of[i] = banks

        def store(i):
            what, s, first, n = strips[i]
            out_sb = out_pool.tile([P, BATCH, n], F32, tag="out")
            stores = set()
            for turned, (m, first_b, end_b) in zip(turned_of[i], parts_of(i)):
                target = out_sb[:, first_b:end_b, m * P - first : (m + 1) * P - first]
                if first_b == 0:
                    nc.scalar.activation(out=target, in_=turned[:], func=ACT.Copy, scale=inv_beta_col[:, 0:1])
                else:
                    nc.vector.tensor_scalar_mul(out=target, in0=turned[:], scalar1=inv_beta_col[:, 0:1])
                stores.add((first_b, end_b))
            for first_b, end_b in sorted(stores):
                nc.sync.dma_start(out=out_view[:, first_b:end_b, first : first + n], in_=out_sb[:, first_b:end_b, :])

        h_raw = const.tile([P, BATCH, E], BF16)
        for b in range(BATCH):
            nc.sync.dma_start(out=h_raw[:, b, :], in_=h_ffn[b, :, :])
        load_ahead(0)
        out_view = out.rearrange("b l n -> l b n")

        warm = const.tile([P, 1], F32)
        nc.vector.memset(warm[:], 0.0)
        nc.scalar.activation(out=warm[:], in_=warm[:], func=ACT.Silu)

        tiles_g = G // P
        bias_rows = const.tile([P, P], BF16)
        nc.vector.memset(bias_rows[:], 0.0)
        b1_bf16 = const.tile([P, F_PASSES, PACK], BF16)
        nc.scalar.dma_start(out=b1_bf16[:], in_=b1.rearrange("(i p t) -> p i t", p=P, t=PACK))
        beta_bf16 = const.tile([P, 1], BF16)
        nc.scalar.dma_start(out=beta_bf16[:], in_=beta.partition_broadcast(P))
        nc.scalar.dma_start(out=bias_rows[0:tiles_g, :], in_=bg.rearrange("(m p) -> m p", p=P))
        nc.scalar.dma_start(out=bias_rows[tiles_g : 2 * tiles_g, :], in_=bl.rearrange("(m p) -> m p", p=P))

        ident_f32 = const.tile([P, P], F32)
        make_identity(nc, ident_f32[:])
        ident_bf16 = const.tile([P, P], BF16)
        make_identity(nc, ident_bf16[:])

        h_grouped = grouped_pool.tile([P, E_PASSES, TOKENS, PACK], BF16, align_bytes=64, tag="grouped")
        h_pairs = h_grouped[:].rearrange("p c r t -> p c (r t)").bitcast(F32).rearrange("p c (r v) -> p c r v", v=PAIR)
        for b in range(BATCH):
            pairs = h_raw[:, b, :].bitcast(F32)
            for c in range(E_PASSES):
                h_t = psum.tile([P, PAIR, P], F32, tag="bank")
                w0 = c * K_PASS // PAIR
                for v in range(PAIR):
                    nc.tensor.transpose(
                        out=h_t[:, v, :], in_=pairs[:, w0 + v : w0 + K_PASS // PAIR : PAIR], identity=ident_f32[:]
                    )
                copy = nc.vector.tensor_copy if c == 0 else nc.scalar.copy
                copy(out=h_pairs[:, c, b * P : (b + 1) * P, :], in_=h_t[:].rearrange("p v r -> p r v"))
        h_words = const.tile([P, E_PASSES, TOKENS], U32, align_bytes=64)
        h_scales = const.tile([P, E_PASSES, TOKENS], U8, align_bytes=64)
        nc.vector.quantize_mx(
            out=h_words[:].rearrange("p c r -> p (c r)").bitcast(FP8X4),
            scales=h_scales[:].rearrange("p c r -> p (c r)"),
            in_=h_grouped[:].rearrange("p c r t -> p (c r t)"),
        )

        bias_t = psum.tile([P, P], BF16, tag="bank")
        nc.tensor.transpose(out=bias_t[:], in_=bias_rows[:], identity=ident_bf16[:])
        bias_cols = const.tile([P, 2 * tiles_g], F32)
        nc.scalar.copy(out=bias_cols[:], in_=bias_t[:, 0 : 2 * tiles_g])
        b1_cols = const.tile([P, F_PASSES * PACK], F32)
        nc.gpsimd.tensor_copy(out=b1_cols[:], in_=b1_bf16[:].rearrange("p i t -> p (i t)"))
        bg_cols = bias_cols[:, 0:tiles_g]
        bl_cols = bias_cols[:, tiles_g : 2 * tiles_g]
        beta_f32 = const.tile([P, 1], F32)
        nc.gpsimd.tensor_copy(out=beta_f32[:], in_=beta_bf16[:])
        beta_sign = const.tile([P, 1], F32)
        nc.gpsimd.tensor_scalar(out=beta_sign[:], in0=beta_f32[:], scalar1=0.0, scalar2=2.0, op0=ALU.is_ge, op1=ALU.mult)
        nc.gpsimd.tensor_scalar(out=beta_sign[:], in0=beta_sign[:], scalar1=1.0, scalar2=-1.0, op0=ALU.mult, op1=ALU.add)
        beta_abs = const.tile([P, 1], F32)
        nc.gpsimd.tensor_tensor(out=beta_abs[:], in0=beta_f32[:], in1=beta_sign[:], op=ALU.mult)
        nc.gpsimd.tensor_scalar(
            out=beta_abs[:], in0=beta_abs[:], scalar1=2.0**-30, scalar2=2.0**64, op0=ALU.max, op1=ALU.min
        )
        beta_col = const.tile([P, 1], F32)
        nc.gpsimd.tensor_tensor(out=beta_col[:], in0=beta_abs[:], in1=beta_sign[:], op=ALU.mult)
        inv_beta_col = const.tile([P, 1], F32)
        beta_bg_cols = const.tile([P, tiles_g], F32)
        nc.gpsimd.tensor_scalar(
            out=beta_bg_cols[:], in0=bg_cols, scalar1=beta_col[:, 0:1], scalar2=0.0, op0=ALU.mult, op1=ALU.add
        )

        u_words = const.tile([P, F_PASSES, TOKENS], U32, align_bytes=64)
        u_scales = const.tile([P, F_PASSES, TOKENS], U8, align_bytes=64)

        first_lin = min(i for i in range(n_strips) if kind(i) == "lin")
        for step in range(n_strips + TURN_LAG):
            if step == first_lin:
                nc.vector.reciprocal(out=inv_beta_col[:], in_=beta_col[:])
            if kind(step - TURN_LAG) == "lin":
                turn(step - TURN_LAG)
            if kind(step) != "none":
                regroup(step)
            if kind(step - SILU_LAG) == "gate":
                silu(step - SILU_LAG)
            if kind(step - TURN_LAG) == "lin":
                store(step - TURN_LAG)
            if kind(step) != "none":
                regroup_on_gpsimd(step)
                load_ahead(step + 1)
            if kind(step - FINISH_LAG) == "u":
                add_bias(step - FINISH_LAG)
            if kind(step - FINISH_LAG) == "lin":
                gated(step - FINISH_LAG)
            if kind(step - QUANTISE_LAG) != "none":
                quantise(step - QUANTISE_LAG)
            if kind(step - FINISH_LAG) == "u":
                quantise_u(step - FINISH_LAG)
            if kind(step - MULTIPLY_LAG) != "none":
                multiply(step - MULTIPLY_LAG)
